import numpy as np
import ml_dtypes


def mxq(x, axis, fmt="e4m3"):
    dtype, down = {"e4m3": (ml_dtypes.float8_e4m3fn, 7), "e5m2": (ml_dtypes.float8_e5m2, 14)}[fmt]
    v = np.moveaxis(np.asarray(x, np.float32).astype(ml_dtypes.bfloat16).astype(np.float64), axis, -1)
    blocks = v.reshape(v.shape[:-1] + (-1, 32))
    amax = np.abs(blocks).max(-1, keepdims=True)
    byte = np.maximum(np.where(amax > 0, np.frexp(amax)[1] - 1 + 127, 0) - down, 1)
    scale = np.exp2(byte - 127.0)
    codes = (blocks / scale).astype(np.float32).astype(dtype).astype(np.float64)
    return np.moveaxis((codes * scale).reshape(v.shape), -1, axis)


WIDE = False


def mx_kscale(k):
    if not WIDE:
        return np.ones(k)
    levels = np.array([10, -10, 5, -5, 0])
    if k % 512:
        return np.exp2(np.random.permutation(np.resize(levels, k // 32))).repeat(32)
    a = np.empty((k // 512, 16))
    for p in range(k // 512):
        a[p, :8] = np.random.permutation(np.resize(levels, 8))
        for g in range(8):
            far = levels[np.abs(levels - a[p, g]) >= 10]
            a[p, g + 8] = far[np.random.randint(len(far))]
    return np.exp2(a.ravel()).repeat(32)


BF16 = ml_dtypes.bfloat16


def bf(x):
    return np.asarray(x, np.float32).astype(BF16)


def f64(x):
    return np.asarray(x).astype(np.float64)


B, SQ, SK, D, DK, L = 2, 4096, 4096, 2048, 64, 10000
P = max(SQ, SK)


def setup_inputs():
    s, t = mx_kscale(D), mx_kscale(D)
    return {"pe": bf(np.random.standard_normal((P, D)) * s),
            "Uq": bf(np.random.standard_normal((D, D)) * 0.6 / np.sqrt(D) / s[:, None] * t),
            "Uk": bf(np.random.standard_normal((D, D)) * 0.6 / np.sqrt(D) / s[:, None] / t)}


def reference(pe, Uq, Uk):
    peq = mxq(f64(pe), 1, "e4m3")
    q_pe = peq[:SQ] @ mxq(f64(Uq), 0, "e4m3")
    k_pe = peq[:SK] @ mxq(f64(Uk), 0, "e4m3")
    return mxq(q_pe, 1, "e4m3") @ mxq(k_pe, 1, "e4m3").T

@@ -1,0 +1,290 @@
+from contextlib import ExitStack
+
+import concourse.mybir as mybir
+from concourse.masks import make_identity
+
+FLOPS = 2 * 2 * 4096 * 2048 * 2048 + 2 * 4096 * 4096 * 2048
+
+F32 = mybir.dt.float32
+BF16 = mybir.dt.bfloat16
+U32 = mybir.dt.uint32
+U8 = mybir.dt.uint8
+FP8X4 = mybir.dt.float8_e4m3fn_x4
+
+P = 128
+CH = 512
+NCHUNK = 8
+NPASS = 4
+NGROUP = 4
+
+
+def tile_multiheadattention_tupe_pa_l_kernel(tc, pe, Uq, Uk, out):
+    nc = tc.nc
+    weights = (Uk, Uq)
+
+    with ExitStack() as ctx:
+        sb = ctx.enter_context(tc.tile_pool(name="sb", bufs=1))
+        ps = ctx.enter_context(tc.psum_pool(name="ps", bufs=8))
+
+        def sbuf(shape, dtype, tag, bufs, name):
+            return sb.tile(shape, dtype, tag=tag, bufs=bufs, name=name, align_bytes=64)
+
+        def new_bank(name):
+            return ps.tile([P, CH], F32, tag="bank", bufs=8, name=name)
+
+        ident = sbuf([P, P], F32, "ident", 1, "ident")
+        make_identity(nc, ident[:])
+
+        ctx.enter_context(tc.manual_schedule())
+
+        pe_raw = {}
+        pe_bank = {}
+        pe_grp = {}
+        pq_codes = {}
+        pq_scales = {}
+        u_raw = {}
+        u_grp = {}
+        u_codes = {}
+        u_scales = {}
+        s1_bank = {}
+        s1_rows = {}
+        s1_grp = {}
+        k_codes = {}
+        k_scales = {}
+
+        def load_pe(n, g):
+            t = sbuf([P, 4, CH], BF16, "pe_raw", 8, "peraw_%d_%d" % (n, g))
+            nc.sync.dma_start(
+                out=t[:],
+                in_=pe[CH * n : CH * (n + 1), CH * g : CH * (g + 1)].rearrange("(r p) k -> p r k", p=P),
+            )
+            pe_raw[(n, g)] = t
+
+        def transpose_pe(n, g):
+            words = pe_raw.pop((n, g))[:].rearrange("p r k -> p (r k)").bitcast(F32)
+            for b in range(2):
+                bank = new_bank("trb_%d_%d_%d" % (n, g, b))
+                for u in range(2):
+                    for rr in range(2):
+                        r = 2 * b + rr
+                        s = 2 * u + rr
+                        nc.tensor.transpose(
+                            bank[:, P * s : P * (s + 1)],
+                            words[:, 256 * r + u : 256 * (r + 1) : 2],
+                            ident[:],
+                        )
+                pe_bank[(n, g, b)] = bank
+
+        def evac_pe(n, g):
+            grp = sbuf([P, 4 * CH], BF16, "pe_grp", 4, "pegrp_%d_%d" % (n, g))
+            gw = grp[:].bitcast(F32)
+            for b in range(2):
+                bank = pe_bank.pop((n, g, b))
+                nc.scalar.copy(
+                    out=gw[:, CH * b : CH * (b + 1)].rearrange("p (w u) -> p w u", u=2),
+                    in_=bank[:].rearrange("p (u w) -> p w u", u=2),
+                )
+            pe_grp[(n, g)] = grp
+
+        def new_pq(key, name):
+            pq_codes[key] = sbuf([P, NPASS, CH], U32, "pq_codes", 9, "c_%s" % name)
+            pq_scales[key] = sbuf([P, CH], U8, "pq_scales", 9, "s_%s" % name)
+
+        def quant_pe(n, g):
+            if g == 0:
+                new_pq(("pe", n), "pe%d" % n)
+            nc.vector.quantize_mx(
+                out=pq_codes[("pe", n)][:, g, :].bitcast(FP8X4),
+                scales=pq_scales[("pe", n)][4 * g : P, :],
+                in_=pe_grp.pop((n, g))[:],
+            )
+
+        def tr_pair(n, gs):
+            for g in gs:
+                transpose_pe(n, g)
+            for g in gs:
+                evac_pe(n, g)
+            if n + 2 < NCHUNK:
+                for g in gs:
+                    load_pe(n + 2, g)
+
+        def load_u(grp_i, g):
+            w = weights[grp_i // NGROUP]
+            c = grp_i % NGROUP
+            t = sbuf([P, 4, CH], BF16, "io", 5, "uraw_%d_%d" % (grp_i, g))
+            nc.sync.dma_start(
+                out=t[:],
+                in_=w[CH * g : CH * (g + 1), CH * c : CH * (c + 1)].rearrange("(p j) c -> p j c", j=4),
+            )
+            u_raw[(grp_i, g)] = t
+
+        def copy_u(grp_i, g):
+            grp = sbuf([P, 4 * CH], BF16, "grp", 3, "ugrp_%d_%d" % (grp_i, g))
+            nc.vector.tensor_copy(
+                out=grp[:].rearrange("p (t m j) -> p t m j", t=4, j=4),
+                in_=u_raw.pop((grp_i, g))[:].rearrange("p j (m t) -> p t m j", t=4),
+            )
+            u_grp[(grp_i, g)] = grp
+
+        def quant_u(grp_i, g):
+            if g == 0:
+                u_codes[grp_i] = sbuf([P, NPASS, CH], U32, "u_codes", 5, "uc_%d" % grp_i)
+                u_scales[grp_i] = sbuf([P, CH], U8, "u_scales", 5, "us_%d" % grp_i)
+            nc.vector.quantize_mx(
+                out=u_codes[grp_i][:, g, :].bitcast(FP8X4),
+                scales=u_scales[grp_i][4 * g : P, :],
+                in_=u_grp.pop((grp_i, g))[:],
+            )
+
+        def s1_banks(grp_i, n, ts):
+            for t in ts:
+                bank = new_bank("s1b_%d_%d_%d" % (grp_i, n, t))
+                for g in range(NPASS):
+                    nc.tensor.matmul_mx(
+                        out=bank[:],
+                        lhsT=u_codes[grp_i][:, g, P * t : P * (t + 1)].bitcast(FP8X4),
+                        lhsT_scale=u_scales[grp_i][4 * g : P, P * t : P * (t + 1)],
+                        rhs=pq_codes[("pe", n)][:, g, :].bitcast(FP8X4),
+                        rhs_scale=pq_scales[("pe", n)][4 * g : P, :],
+                        start=(g == 0),
+                        stop=(g == NPASS - 1),
+                    )
+                if t == 0:
+                    s1_rows[(grp_i, n)] = sbuf([P, 4, CH], BF16, "s1_rows", 3, "s1r_%d_%d" % (grp_i, n))
+                nc.scalar.copy(out=s1_rows[(grp_i, n)][:, t, :], in_=bank[:])
+
+        def s1_copy(grp_i, n):
+            grp = sbuf([P, 4 * CH], BF16, "grp", 3, "s1g_%d_%d" % (grp_i, n))
+            nc.vector.tensor_copy(
+                out=grp[:].rearrange("p (w t) -> p w t", t=4),
+                in_=s1_rows.pop((grp_i, n))[:].rearrange("p t w -> p w t"),
+            )
+            s1_grp[(grp_i, n)] = grp
+
+        def k_tile(c, h):
+            if c == 0:
+                return sbuf([P, 2, CH], U32, "k0_codes", 4, "kc_%d_%d" % (c, h))
+            if c == 3:
+                return sbuf([P, 2, CH], U32, "pe_grp", 4, "kc_%d_%d" % (c, h))
+            return sbuf([P, 2, CH], U32, "pe_raw", 8, "kc_%d_%d" % (c, h))
+
+        def s1_quant(grp_i, n):
+            c = grp_i % NGROUP
+            if grp_i < NGROUP:
+                if n % 2 == 0:
+                    k_codes[(c, n // 2)] = k_tile(c, n // 2)
+                if c == 0:
+                    k_scales[n] = sbuf([P, CH], U8, "k_scales", 8, "ks_%d" % n)
+                codes = k_codes[(c, n // 2)][:, n % 2, :]
+                scales = k_scales[n]
+            else:
+                if c == 0:
+                    new_pq(("q", n), "q%d" % n)
+                codes = pq_codes[("q", n)][:, c, :]
+                scales = pq_scales[("q", n)]
+            nc.vector.quantize_mx(
+                out=codes.bitcast(FP8X4),
+                scales=scales[4 * c : P, :],
+                in_=s1_grp.pop((grp_i, n))[:],
+            )
+
+        def s2_tile(i):
+            n = i // 4
+            r = i % 4
+            rows = None
+            for j in range(NCHUNK):
+                bank = new_bank("s2b_%d_%d" % (i, j))
+                for c in range(NPASS):
+                    nc.tensor.matmul_mx(
+                        out=bank[:],
+                        lhsT=pq_codes[("q", n)][:, c, P * r : P * (r + 1)].bitcast(FP8X4),
+                        lhsT_scale=pq_scales[("q", n)][4 * c : P, P * r : P * (r + 1)],
+                        rhs=k_codes[(c, j // 2)][:, j % 2, :].bitcast(FP8X4),
+                        rhs_scale=k_scales[j][4 * c : P, :],
+                        start=(c == 0),
+                        stop=(c == NPASS - 1),
+                    )
+                if j % 2 == 0:
+                    rows = sbuf([P, 2 * CH], F32, "io", 5, "o_%d_%d" % (i, j))
+                    nc.scalar.copy(out=rows[:, 0:CH], in_=bank[:])
+                else:
+                    nc.vector.tensor_copy(out=rows[:, CH : 2 * CH], in_=bank[:])
+                    nc.sync.dma_start(out=out[P * i : P * (i + 1), CH * (j - 1) : CH * (j + 1)], in_=rows[:])
+
+        items = [(grp_i, g) for grp_i in range(1, 2 * NGROUP) for g in range(NPASS)]
+
+        def item_copy(x):
+            if x < len(items):
+                copy_u(items[x][0], items[x][1])
+                if x + 3 < len(items):
+                    load_u(items[x + 3][0], items[x + 3][1])
+
+        def item_quant(x):
+            if x < len(items):
+                quant_u(items[x][0], items[x][1])
+
+        for g in range(NPASS):
+            load_pe(0, g)
+            load_u(0, g)
+        for g in range(NPASS):
+            load_pe(1, g)
+        for x in range(3):
+            load_u(items[x][0], items[x][1])
+
+        tr_pair(0, (0, 1))
+        copy_u(0, 0)
+        copy_u(0, 1)
+        quant_u(0, 0)
+        quant_u(0, 1)
+        quant_pe(0, 0)
+        quant_pe(0, 1)
+        tr_pair(0, (2, 3))
+        copy_u(0, 2)
+        copy_u(0, 3)
+        quant_u(0, 2)
+        quant_pe(0, 2)
+        quant_u(0, 3)
+        quant_pe(0, 3)
+        tr_pair(1, (0, 1))
+        quant_pe(1, 0)
+        quant_pe(1, 1)
+
+        for n in range(NCHUNK):
+            s1_banks(0, n, (0, 1))
+            if n + 1 < NCHUNK:
+                tr_pair(n + 1, (2, 3))
+                quant_pe(n + 1, 2)
+                quant_pe(n + 1, 3)
+            item_copy(n)
+            s1_banks(0, n, (2, 3))
+            s1_copy(0, n)
+            item_quant(n)
+            s1_quant(0, n)
+            if n + 2 < NCHUNK:
+                tr_pair(n + 2, (0, 1))
+                quant_pe(n + 2, 0)
+                quant_pe(n + 2, 1)
+
+        for x in range(NCHUNK, NGROUP * NCHUNK):
+            c = x // NCHUNK
+            n = x % NCHUNK
+            s1_banks(c, n, (0, 1, 2, 3))
+            item_copy(x)
+            s1_copy(c, n)
+            item_quant(x)
+            s1_quant(c, n)
+
+        def q_unit(idx):
+            n = idx // NGROUP
+            c = idx % NGROUP
+            s1_banks(NGROUP + c, n, (0, 1, 2, 3))
+            s1_copy(NGROUP + c, n)
+            s1_quant(NGROUP + c, n)
+
+        lead = NGROUP + 1
+        for idx in range(lead):
+            q_unit(idx)
+        for i in range(4 * NCHUNK):
+            s2_tile(i)
+            if i + lead < NGROUP * NCHUNK:
+                q_unit(i + lead)

@@ -88,14 +88,23 @@ def tile_multiheadattention_tupe_pa_l_kernel(tc, pe, Uq, Uk, out):
 
         def new_pq(key, name):
             pq_codes[key] = sbuf([P, NPASS, CH], U32, "pq_codes", 9, "c_%s" % name)
-            pq_scales[key] = sbuf([P, CH], U8, "pq_scales", 9, "s_%s" % name)
+            pq_scales[key] = sbuf([P, CH], U8, "pq_scales", 12, "s_%s" % name)
+
+        def pe_scale(n, g):
+            if n == 0:
+                return pq_scales[("pe0", g)][:, :]
+            return pq_scales[("pe", n)][4 * g : P, :]
 
         def quant_pe(n, g):
             if g == 0:
                 new_pq(("pe", n), "pe%d" % n)
+            if n == 0 and g > 0:
+                pq_scales[("pe0", g)] = sbuf([P, CH], U8, "pq_scales", 12, "s_pe0_%d" % g)
+            if n == 0 and g == 0:
+                pq_scales[("pe0", 0)] = pq_scales[("pe", 0)]
             nc.vector.quantize_mx(
                 out=pq_codes[("pe", n)][:, g, :].bitcast(FP8X4),
-                scales=pq_scales[("pe", n)][4 * g : P, :],
+                scales=pe_scale(n, g),
                 in_=pe_grp.pop((n, g))[:],
             )
 
@@ -118,43 +127,62 @@ def tile_multiheadattention_tupe_pa_l_kernel(tc, pe, Uq, Uk, out):
             )
             u_raw[(grp_i, g)] = t
 
-        def copy_u(grp_i, g):
-            grp = sbuf([P, 4 * CH], BF16, "grp", 3, "ugrp_%d_%d" % (grp_i, g))
-            nc.vector.tensor_copy(
-                out=grp[:].rearrange("p (t m j) -> p t m j", t=4, j=4),
-                in_=u_raw.pop((grp_i, g))[:].rearrange("p j (m t) -> p t m j", t=4),
-            )
+        def copy_u(grp_i, g, on_scalar):
+            grp = sbuf([P, 4 * CH], BF16, "grp", 4, "ugrp_%d_%d" % (grp_i, g))
+            dst = grp[:].rearrange("p (t m j) -> p t m j", t=4, j=4)
+            src = u_raw.pop((grp_i, g))[:].rearrange("p j (m t) -> p t m j", t=4)
+            if on_scalar:
+                nc.scalar.copy(out=dst, in_=src)
+            else:
+                nc.vector.tensor_copy(out=dst, in_=src)
             u_grp[(grp_i, g)] = grp
+
+        def u_scale(grp_i, g, lo, hi):
+            if grp_i == 0:
+                return u_scales[(0, g)][:, lo:hi]
+            return u_scales[(grp_i, 0)][4 * g : P, lo:hi]
 
         def quant_u(grp_i, g):
             if g == 0:
                 u_codes[grp_i] = sbuf([P, NPASS, CH], U32, "u_codes", 5, "uc_%d" % grp_i)
-                u_scales[grp_i] = sbuf([P, CH], U8, "u_scales", 5, "us_%d" % grp_i)
+            if g == 0 or grp_i == 0:
+                u_scales[(grp_i, g)] = sbuf([P, CH], U8, "u_scales", 8, "us_%d_%d" % (grp_i, g))
             nc.vector.quantize_mx(
                 out=u_codes[grp_i][:, g, :].bitcast(FP8X4),
-                scales=u_scales[grp_i][4 * g : P, :],
+                scales=u_scale(grp_i, g, 0, CH),
                 in_=u_grp.pop((grp_i, g))[:],
             )
 
-        def s1_banks(grp_i, n, ts):
-            for t in ts:
-                bank = new_bank("s1b_%d_%d_%d" % (grp_i, n, t))
-                for g in range(NPASS):
-                    nc.tensor.matmul_mx(
-                        out=bank[:],
-                        lhsT=u_codes[grp_i][:, g, P * t : P * (t + 1)].bitcast(FP8X4),
-                        lhsT_scale=u_scales[grp_i][4 * g : P, P * t : P * (t + 1)],
-                        rhs=pq_codes[("pe", n)][:, g, :].bitcast(FP8X4),
-                        rhs_scale=pq_scales[("pe", n)][4 * g : P, :],
-                        start=(g == 0),
-                        stop=(g == NPASS - 1),
-                    )
-                if t == 0:
-                    s1_rows[(grp_i, n)] = sbuf([P, 4, CH], BF16, "s1_rows", 3, "s1r_%d_%d" % (grp_i, n))
+        def s1_pass(grp_i, n, t, g):
+            if g == 0:
+                s1_bank[(grp_i, n, t)] = new_bank("s1b_%d_%d_%d" % (grp_i, n, t))
+            nc.tensor.matmul_mx(
+                out=s1_bank[(grp_i, n, t)][:],
+                lhsT=u_codes[grp_i][:, g, P * t : P * (t + 1)].bitcast(FP8X4),
+                lhsT_scale=u_scale(grp_i, g, P * t, P * (t + 1)),
+                rhs=pq_codes[("pe", n)][:, g, :].bitcast(FP8X4),
+                rhs_scale=pe_scale(n, g),
+                start=(g == 0),
+                stop=(g == NPASS - 1),
+            )
+
+        def s1_evac(grp_i, n, t, on_vector):
+            if t == 0:
+                s1_rows[(grp_i, n)] = sbuf([P, 4, CH], BF16, "s1_rows", 2, "s1r_%d_%d" % (grp_i, n))
+            bank = s1_bank.pop((grp_i, n, t))
+            if on_vector:
+                nc.vector.tensor_copy(out=s1_rows[(grp_i, n)][:, t, :], in_=bank[:])
+            else:
                 nc.scalar.copy(out=s1_rows[(grp_i, n)][:, t, :], in_=bank[:])
 
+        def s1_banks(grp_i, n, ts, share):
+            for t in ts:
+                for g in range(NPASS):
+                    s1_pass(grp_i, n, t, g)
+                s1_evac(grp_i, n, t, share and t % 2 == 1)
+
         def s1_copy(grp_i, n):
-            grp = sbuf([P, 4 * CH], BF16, "grp", 3, "s1g_%d_%d" % (grp_i, n))
+            grp = sbuf([P, 4 * CH], BF16, "grp", 4, "s1g_%d_%d" % (grp_i, n))
             nc.vector.tensor_copy(
                 out=grp[:].rearrange("p (w t) -> p w t", t=4),
                 in_=s1_rows.pop((grp_i, n))[:].rearrange("p t w -> p w t"),
@@ -212,53 +240,78 @@ def tile_multiheadattention_tupe_pa_l_kernel(tc, pe, Uq, Uk, out):
                     nc.sync.dma_start(out=out[P * i : P * (i + 1), CH * (j - 1) : CH * (j + 1)], in_=rows[:])
 
         items = [(grp_i, g) for grp_i in range(1, 2 * NGROUP) for g in range(NPASS)]
+        LAG = 2
 
-        def item_copy(x):
-            if x < len(items):
-                copy_u(items[x][0], items[x][1])
-                if x + 3 < len(items):
-                    load_u(items[x + 3][0], items[x + 3][1])
+        def scalar_copies(k):
+            return k % 2 == 1 and k + LAG > NCHUNK
 
-        def item_quant(x):
-            if x < len(items):
-                quant_u(items[x][0], items[x][1])
+        def slot_load(x):
+            if 0 <= x + 1 < len(items):
+                load_u(items[x + 1][0], items[x + 1][1])
+
+        def slot_copy(x):
+            k = x - LAG
+            if 0 <= k < len(items) and not scalar_copies(k):
+                copy_u(items[k][0], items[k][1], False)
+
+        def slot_copy_ahead(x):
+            k = x + 1 - LAG
+            if 0 <= k < len(items) and scalar_copies(k):
+                copy_u(items[k][0], items[k][1], True)
+
+        def slot_quant(x):
+            k = x - LAG
+            if 0 <= k < len(items):
+                quant_u(items[k][0], items[k][1])
 
         for g in range(NPASS):
-            load_pe(0, g)
             load_u(0, g)
+            load_pe(0, g)
         for g in range(NPASS):
             load_pe(1, g)
-        for x in range(3):
-            load_u(items[x][0], items[x][1])
 
-        tr_pair(0, (0, 1))
-        copy_u(0, 0)
-        copy_u(0, 1)
+        tr_pair(0, (0,))
+        copy_u(0, 0, False)
         quant_u(0, 0)
-        quant_u(0, 1)
-        quant_pe(0, 0)
-        quant_pe(0, 1)
-        tr_pair(0, (2, 3))
-        copy_u(0, 2)
-        copy_u(0, 3)
-        quant_u(0, 2)
-        quant_pe(0, 2)
-        quant_u(0, 3)
-        quant_pe(0, 3)
-        tr_pair(1, (0, 1))
+        for g in range(NPASS):
+            if g + 1 < NPASS:
+                tr_pair(0, (g + 1,))
+                copy_u(0, g + 1, False)
+            else:
+                tr_pair(1, (0, 1))
+            quant_pe(0, g)
+            if g + 1 < NPASS:
+                quant_u(0, g + 1)
+            for t in range(4):
+                s1_pass(0, 0, t, g)
+        for t in range(4):
+            s1_evac(0, 0, t, False)
         quant_pe(1, 0)
         quant_pe(1, 1)
+        tr_pair(1, (2, 3))
+        for x in range(3):
+            load_u(items[x][0], items[x][1])
+        s1_copy(0, 0)
+        quant_pe(1, 2)
+        s1_quant(0, 0)
+        quant_pe(1, 3)
+        tr_pair(2, (0, 1))
+        quant_pe(2, 0)
+        quant_pe(2, 1)
 
-        for n in range(NCHUNK):
-            s1_banks(0, n, (0, 1))
+        for n in range(1, NCHUNK):
+            s1_banks(0, n, (0, 1), False)
             if n + 1 < NCHUNK:
                 tr_pair(n + 1, (2, 3))
                 quant_pe(n + 1, 2)
                 quant_pe(n + 1, 3)
-            item_copy(n)
-            s1_banks(0, n, (2, 3))
+            slot_copy(n)
+            if n >= LAG:
+                slot_load(n)
+            s1_banks(0, n, (2, 3), False)
+            slot_copy_ahead(n)
             s1_copy(0, n)
-            item_quant(n)
+            slot_quant(n)
             s1_quant(0, n)
             if n + 2 < NCHUNK:
                 tr_pair(n + 2, (0, 1))
@@ -268,16 +321,18 @@ def tile_multiheadattention_tupe_pa_l_kernel(tc, pe, Uq, Uk, out):
         for x in range(NCHUNK, NGROUP * NCHUNK):
             c = x // NCHUNK
             n = x % NCHUNK
-            s1_banks(c, n, (0, 1, 2, 3))
-            item_copy(x)
+            s1_banks(c, n, (0, 1, 2, 3), False)
+            slot_copy_ahead(x)
+            slot_copy(x)
+            slot_load(x)
             s1_copy(c, n)
-            item_quant(x)
+            slot_quant(x)
             s1_quant(c, n)
 
         def q_unit(idx):
             n = idx // NGROUP
             c = idx % NGROUP
-            s1_banks(NGROUP + c, n, (0, 1, 2, 3))
+            s1_banks(NGROUP + c, n, (0, 1, 2, 3), True)
             s1_copy(NGROUP + c, n)
             s1_quant(NGROUP + c, n)
 

@@ -16,6 +16,7 @@ CH = 512
 NCHUNK = 8
 NPASS = 4
 NGROUP = 4
+SORT_FROM = 3
 
 
 def tile_multiheadattention_tupe_pa_l_kernel(tc, pe, Uq, Uk, out):
@@ -38,6 +39,7 @@ def tile_multiheadattention_tupe_pa_l_kernel(tc, pe, Uq, Uk, out):
         ctx.enter_context(tc.manual_schedule())
 
         pe_raw = {}
+        pe_srt = {}
         pe_bank = {}
         pe_grp = {}
         pq_codes = {}
@@ -53,26 +55,43 @@ def tile_multiheadattention_tupe_pa_l_kernel(tc, pe, Uq, Uk, out):
         k_scales = {}
 
         def load_pe(n, g):
-            t = sbuf([P, 4, CH], BF16, "pe_raw", 8, "peraw_%d_%d" % (n, g))
+            tag = "pe_raw"
+            if n == 0 or n == 2:
+                tag = "pe_srt"
+            t = sbuf([P, 4, CH], BF16, tag, 4, "peraw_%d_%d" % (n, g))
             nc.sync.dma_start(
                 out=t[:],
                 in_=pe[CH * n : CH * (n + 1), CH * g : CH * (g + 1)].rearrange("(r p) k -> p r k", p=P),
             )
             pe_raw[(n, g)] = t
 
-        def transpose_pe(n, g):
+        def sort_pe(n, g):
             words = pe_raw.pop((n, g))[:].rearrange("p r k -> p (r k)").bitcast(F32)
+            srt = sbuf([P, 2 * CH], F32, "pe_srt", 4, "pesrt_%d_%d" % (n, g))
+            nc.vector.tensor_copy(
+                out=srt[:].rearrange("p (r u m) -> p r u m", r=4, u=2),
+                in_=words.rearrange("p (r m u) -> p r u m", r=4, u=2),
+            )
+            pe_srt[(n, g)] = srt
+            if n + 1 < NCHUNK:
+                load_pe(n + 1, g)
+
+        def transpose_pe(n, g):
+            if n >= SORT_FROM:
+                words = pe_srt.pop((n, g))
+            else:
+                words = pe_raw.pop((n, g))[:].rearrange("p r k -> p (r k)").bitcast(F32)
             for b in range(2):
                 bank = new_bank("trb_%d_%d_%d" % (n, g, b))
                 for u in range(2):
                     for rr in range(2):
                         r = 2 * b + rr
                         s = 2 * u + rr
-                        nc.tensor.transpose(
-                            bank[:, P * s : P * (s + 1)],
-                            words[:, 256 * r + u : 256 * (r + 1) : 2],
-                            ident[:],
-                        )
+                        if n >= SORT_FROM:
+                            src = words[:, 256 * r + P * u : 256 * r + P * (u + 1)]
+                        else:
+                            src = words[:, 256 * r + u : 256 * (r + 1) : 2]
+                        nc.tensor.transpose(bank[:, P * s : P * (s + 1)], src, ident[:])
                 pe_bank[(n, g, b)] = bank
 
         def evac_pe(n, g):
@@ -113,7 +132,7 @@ def tile_multiheadattention_tupe_pa_l_kernel(tc, pe, Uq, Uk, out):
                 transpose_pe(n, g)
             for g in gs:
                 evac_pe(n, g)
-            if n + 2 < NCHUNK:
+            if n + 2 <= SORT_FROM:
                 for g in gs:
                     load_pe(n + 2, g)
 
@@ -194,7 +213,9 @@ def tile_multiheadattention_tupe_pa_l_kernel(tc, pe, Uq, Uk, out):
                 return sbuf([P, 2, CH], U32, "k0_codes", 4, "kc_%d_%d" % (c, h))
             if c == 3:
                 return sbuf([P, 2, CH], U32, "pe_grp", 4, "kc_%d_%d" % (c, h))
-            return sbuf([P, 2, CH], U32, "pe_raw", 8, "kc_%d_%d" % (c, h))
+            if c == 2:
+                return sbuf([P, 2, CH], U32, "pe_srt", 4, "kc_%d_%d" % (c, h))
+            return sbuf([P, 2, CH], U32, "pe_raw", 4, "kc_%d_%d" % (c, h))
 
         def s1_quant(grp_i, n):
             c = grp_i % NGROUP
@@ -240,14 +261,20 @@ def tile_multiheadattention_tupe_pa_l_kernel(tc, pe, Uq, Uk, out):
                     nc.sync.dma_start(out=out[P * i : P * (i + 1), CH * (j - 1) : CH * (j + 1)], in_=rows[:])
 
         items = [(grp_i, g) for grp_i in range(1, 2 * NGROUP) for g in range(NPASS)]
-        LAG = 2
+        LAG = 3
 
         def scalar_copies(k):
             return k % 2 == 1 and k + LAG > NCHUNK
 
         def slot_load(x):
-            if 0 <= x + 1 < len(items):
-                load_u(items[x + 1][0], items[x + 1][1])
+            k = x - LAG + 2
+            if 0 <= k < len(items):
+                load_u(items[k][0], items[k][1])
+
+        def sorts(n, gs):
+            if SORT_FROM <= n < NCHUNK:
+                for g in gs:
+                    sort_pe(n, g)
 
         def slot_copy(x):
             k = x - LAG
@@ -289,8 +316,6 @@ def tile_multiheadattention_tupe_pa_l_kernel(tc, pe, Uq, Uk, out):
         quant_pe(1, 0)
         quant_pe(1, 1)
         tr_pair(1, (2, 3))
-        for x in range(3):
-            load_u(items[x][0], items[x][1])
         s1_copy(0, 0)
         quant_pe(1, 2)
         s1_quant(0, 0)
@@ -300,14 +325,15 @@ def tile_multiheadattention_tupe_pa_l_kernel(tc, pe, Uq, Uk, out):
         quant_pe(2, 1)
 
         for n in range(1, NCHUNK):
+            sorts(n + 2, (0, 1))
             s1_banks(0, n, (0, 1), False)
             if n + 1 < NCHUNK:
                 tr_pair(n + 1, (2, 3))
                 quant_pe(n + 1, 2)
                 quant_pe(n + 1, 3)
             slot_copy(n)
-            if n >= LAG:
-                slot_load(n)
+            slot_load(n)
+            sorts(n + 2, (2, 3))
             s1_banks(0, n, (2, 3), False)
             slot_copy_ahead(n)
             s1_copy(0, n)

@@ -69,8 +69,8 @@ def tile_multiheadattention_tupe_pa_l_kernel(tc, pe, Uq, Uk, out):
             words = pe_raw.pop((n, g))[:].rearrange("p r k -> p (r k)").bitcast(F32)
             srt = sbuf([P, 2 * CH], F32, "pe_srt", 4, "pesrt_%d_%d" % (n, g))
             nc.vector.tensor_copy(
-                out=srt[:].rearrange("p (r u m) -> p r u m", r=4, u=2),
-                in_=words.rearrange("p (r m u) -> p r u m", r=4, u=2),
+                out=srt[:].rearrange("p (r u m) -> p r m u", r=4, u=2),
+                in_=words.rearrange("p (r m u) -> p r m u", r=4, u=2),
             )
             pe_srt[(n, g)] = srt
             if n + 1 < NCHUNK:

from contextlib import ExitStack

import concourse.mybir as mybir
from concourse.masks import make_identity

FLOPS = 2 * 2 * 4096 * 2048 * 2048 + 2 * 4096 * 4096 * 2048

F32 = mybir.dt.float32
BF16 = mybir.dt.bfloat16
U32 = mybir.dt.uint32
U8 = mybir.dt.uint8
FP8X4 = mybir.dt.float8_e4m3fn_x4

P = 128
CH = 512
NCHUNK = 8
NPASS = 4
NGROUP = 4
SORT_FROM = 3


def tile_multiheadattention_tupe_pa_l_kernel(tc, pe, Uq, Uk, out):
    nc = tc.nc
    weights = (Uk, Uq)

    with ExitStack() as ctx:
        sb = ctx.enter_context(tc.tile_pool(name="sb", bufs=1))
        ps = ctx.enter_context(tc.psum_pool(name="ps", bufs=8))

        def sbuf(shape, dtype, tag, bufs, name):
            return sb.tile(shape, dtype, tag=tag, bufs=bufs, name=name, align_bytes=64)

        def new_bank(name):
            return ps.tile([P, CH], F32, tag="bank", bufs=8, name=name)

        ident = sbuf([P, P], F32, "ident", 1, "ident")
        make_identity(nc, ident[:])

        ctx.enter_context(tc.manual_schedule())

        pe_raw = {}
        pe_srt = {}
        pe_bank = {}
        pe_grp = {}
        pq_codes = {}
        pq_scales = {}
        u_raw = {}
        u_grp = {}
        u_codes = {}
        u_scales = {}
        s1_bank = {}
        s1_rows = {}
        s1_grp = {}
        k_codes = {}
        k_scales = {}

        def load_pe(n, g):
            tag = "pe_raw"
            if n == 0 or n == 2:
                tag = "pe_srt"
            t = sbuf([P, 4, CH], BF16, tag, 4, "peraw_%d_%d" % (n, g))
            nc.sync.dma_start(
                out=t[:],
                in_=pe[CH * n : CH * (n + 1), CH * g : CH * (g + 1)].rearrange("(r p) k -> p r k", p=P),
            )
            pe_raw[(n, g)] = t

        def sort_pe(n, g):
            words = pe_raw.pop((n, g))[:].rearrange("p r k -> p (r k)").bitcast(F32)
            srt = sbuf([P, 2 * CH], F32, "pe_srt", 4, "pesrt_%d_%d" % (n, g))
            nc.vector.tensor_copy(
                out=srt[:].rearrange("p (r u m) -> p r m u", r=4, u=2),
                in_=words.rearrange("p (r m u) -> p r m u", r=4, u=2),
            )
            pe_srt[(n, g)] = srt
            if n + 1 < NCHUNK:
                load_pe(n + 1, g)

        def transpose_pe(n, g):
            if n >= SORT_FROM:
                words = pe_srt.pop((n, g))
            else:
                words = pe_raw.pop((n, g))[:].rearrange("p r k -> p (r k)").bitcast(F32)
            for b in range(2):
                bank = new_bank("trb_%d_%d_%d" % (n, g, b))
                for u in range(2):
                    for rr in range(2):
                        r = 2 * b + rr
                        s = 2 * u + rr
                        if n >= SORT_FROM:
                            src = words[:, 256 * r + P * u : 256 * r + P * (u + 1)]
                        else:
                            src = words[:, 256 * r + u : 256 * (r + 1) : 2]
                        nc.tensor.transpose(bank[:, P * s : P * (s + 1)], src, ident[:])
                pe_bank[(n, g, b)] = bank

        def evac_pe(n, g):
            grp = sbuf([P, 4 * CH], BF16, "pe_grp", 4, "pegrp_%d_%d" % (n, g))
            gw = grp[:].bitcast(F32)
            for b in range(2):
                bank = pe_bank.pop((n, g, b))
                nc.scalar.copy(
                    out=gw[:, CH * b : CH * (b + 1)].rearrange("p (w u) -> p w u", u=2),
                    in_=bank[:].rearrange("p (u w) -> p w u", u=2),
                )
            pe_grp[(n, g)] = grp

        def new_pq(key, name):
            pq_codes[key] = sbuf([P, NPASS, CH], U32, "pq_codes", 9, "c_%s" % name)
            pq_scales[key] = sbuf([P, CH], U8, "pq_scales", 12, "s_%s" % name)

        def pe_scale(n, g):
            if n == 0:
                return pq_scales[("pe0", g)][:, :]
            return pq_scales[("pe", n)][4 * g : P, :]

        def quant_pe(n, g):
            if g == 0:
                new_pq(("pe", n), "pe%d" % n)
            if n == 0 and g > 0:
                pq_scales[("pe0", g)] = sbuf([P, CH], U8, "pq_scales", 12, "s_pe0_%d" % g)
            if n == 0 and g == 0:
                pq_scales[("pe0", 0)] = pq_scales[("pe", 0)]
            nc.vector.quantize_mx(
                out=pq_codes[("pe", n)][:, g, :].bitcast(FP8X4),
                scales=pe_scale(n, g),
                in_=pe_grp.pop((n, g))[:],
            )

        def tr_pair(n, gs):
            for g in gs:
                transpose_pe(n, g)
            for g in gs:
                evac_pe(n, g)
            if n + 2 <= SORT_FROM:
                for g in gs:
                    load_pe(n + 2, g)

        def load_u(grp_i, g):
            w = weights[grp_i // NGROUP]
            c = grp_i % NGROUP
            t = sbuf([P, 4, CH], BF16, "io", 5, "uraw_%d_%d" % (grp_i, g))
            nc.sync.dma_start(
                out=t[:],
                in_=w[CH * g : CH * (g + 1), CH * c : CH * (c + 1)].rearrange("(p j) c -> p j c", j=4),
            )
            u_raw[(grp_i, g)] = t

        def copy_u(grp_i, g, on_scalar):
            grp = sbuf([P, 4 * CH], BF16, "grp", 4, "ugrp_%d_%d" % (grp_i, g))
            dst = grp[:].rearrange("p (t m j) -> p t m j", t=4, j=4)
            src = u_raw.pop((grp_i, g))[:].rearrange("p j (m t) -> p t m j", t=4)
            if on_scalar:
                nc.scalar.copy(out=dst, in_=src)
            else:
                nc.vector.tensor_copy(out=dst, in_=src)
            u_grp[(grp_i, g)] = grp

        def u_scale(grp_i, g, lo, hi):
            if grp_i == 0:
                return u_scales[(0, g)][:, lo:hi]
            return u_scales[(grp_i, 0)][4 * g : P, lo:hi]

        def quant_u(grp_i, g):
            if g == 0:
                u_codes[grp_i] = sbuf([P, NPASS, CH], U32, "u_codes", 5, "uc_%d" % grp_i)
            if g == 0 or grp_i == 0:
                u_scales[(grp_i, g)] = sbuf([P, CH], U8, "u_scales", 8, "us_%d_%d" % (grp_i, g))
            nc.vector.quantize_mx(
                out=u_codes[grp_i][:, g, :].bitcast(FP8X4),
                scales=u_scale(grp_i, g, 0, CH),
                in_=u_grp.pop((grp_i, g))[:],
            )

        def s1_pass(grp_i, n, t, g):
            if g == 0:
                s1_bank[(grp_i, n, t)] = new_bank("s1b_%d_%d_%d" % (grp_i, n, t))
            nc.tensor.matmul_mx(
                out=s1_bank[(grp_i, n, t)][:],
                lhsT=u_codes[grp_i][:, g, P * t : P * (t + 1)].bitcast(FP8X4),
                lhsT_scale=u_scale(grp_i, g, P * t, P * (t + 1)),
                rhs=pq_codes[("pe", n)][:, g, :].bitcast(FP8X4),
                rhs_scale=pe_scale(n, g),
                start=(g == 0),
                stop=(g == NPASS - 1),
            )

        def s1_evac(grp_i, n, t, on_vector):
            if t == 0:
                s1_rows[(grp_i, n)] = sbuf([P, 4, CH], BF16, "s1_rows", 2, "s1r_%d_%d" % (grp_i, n))
            bank = s1_bank.pop((grp_i, n, t))
            if on_vector:
                nc.vector.tensor_copy(out=s1_rows[(grp_i, n)][:, t, :], in_=bank[:])
            else:
                nc.scalar.copy(out=s1_rows[(grp_i, n)][:, t, :], in_=bank[:])

        def s1_banks(grp_i, n, ts, share):
            for t in ts:
                for g in range(NPASS):
                    s1_pass(grp_i, n, t, g)
                s1_evac(grp_i, n, t, share and t % 2 == 1)

        def s1_copy(grp_i, n):
            grp = sbuf([P, 4 * CH], BF16, "grp", 4, "s1g_%d_%d" % (grp_i, n))
            nc.vector.tensor_copy(
                out=grp[:].rearrange("p (w t) -> p w t", t=4),
                in_=s1_rows.pop((grp_i, n))[:].rearrange("p t w -> p w t"),
            )
            s1_grp[(grp_i, n)] = grp

        def k_tile(c, h):
            if c == 0:
                return sbuf([P, 2, CH], U32, "k0_codes", 4, "kc_%d_%d" % (c, h))
            if c == 3:
                return sbuf([P, 2, CH], U32, "pe_grp", 4, "kc_%d_%d" % (c, h))
            if c == 2:
                return sbuf([P, 2, CH], U32, "pe_srt", 4, "kc_%d_%d" % (c, h))
            return sbuf([P, 2, CH], U32, "pe_raw", 4, "kc_%d_%d" % (c, h))

        def s1_quant(grp_i, n):
            c = grp_i % NGROUP
            if grp_i < NGROUP:
                if n % 2 == 0:
                    k_codes[(c, n // 2)] = k_tile(c, n // 2)
                if c == 0:
                    k_scales[n] = sbuf([P, CH], U8, "k_scales", 8, "ks_%d" % n)
                codes = k_codes[(c, n // 2)][:, n % 2, :]
                scales = k_scales[n]
            else:
                if c == 0:
                    new_pq(("q", n), "q%d" % n)
                codes = pq_codes[("q", n)][:, c, :]
                scales = pq_scales[("q", n)]
            nc.vector.quantize_mx(
                out=codes.bitcast(FP8X4),
                scales=scales[4 * c : P, :],
                in_=s1_grp.pop((grp_i, n))[:],
            )

        def s2_tile(i):
            n = i // 4
            r = i % 4
            rows = None
            for j in range(NCHUNK):
                bank = new_bank("s2b_%d_%d" % (i, j))
                for c in range(NPASS):
                    nc.tensor.matmul_mx(
                        out=bank[:],
                        lhsT=pq_codes[("q", n)][:, c, P * r : P * (r + 1)].bitcast(FP8X4),
                        lhsT_scale=pq_scales[("q", n)][4 * c : P, P * r : P * (r + 1)],
                        rhs=k_codes[(c, j // 2)][:, j % 2, :].bitcast(FP8X4),
                        rhs_scale=k_scales[j][4 * c : P, :],
                        start=(c == 0),
                        stop=(c == NPASS - 1),
                    )
                if j % 2 == 0:
                    rows = sbuf([P, 2 * CH], F32, "io", 5, "o_%d_%d" % (i, j))
                    nc.scalar.copy(out=rows[:, 0:CH], in_=bank[:])
                else:
                    nc.vector.tensor_copy(out=rows[:, CH : 2 * CH], in_=bank[:])
                    nc.sync.dma_start(out=out[P * i : P * (i + 1), CH * (j - 1) : CH * (j + 1)], in_=rows[:])

        items = [(grp_i, g) for grp_i in range(1, 2 * NGROUP) for g in range(NPASS)]
        LAG = 3

        def scalar_copies(k):
            return k % 2 == 1 and k + LAG > NCHUNK

        def slot_load(x):
            k = x - LAG + 2
            if 0 <= k < len(items):
                load_u(items[k][0], items[k][1])

        def sorts(n, gs):
            if SORT_FROM <= n < NCHUNK:
                for g in gs:
                    sort_pe(n, g)

        def slot_copy(x):
            k = x - LAG
            if 0 <= k < len(items) and not scalar_copies(k):
                copy_u(items[k][0], items[k][1], False)

        def slot_copy_ahead(x):
            k = x + 1 - LAG
            if 0 <= k < len(items) and scalar_copies(k):
                copy_u(items[k][0], items[k][1], True)

        def slot_quant(x):
            k = x - LAG
            if 0 <= k < len(items):
                quant_u(items[k][0], items[k][1])

        for g in range(NPASS):
            load_u(0, g)
            load_pe(0, g)
        for g in range(NPASS):
            load_pe(1, g)

        tr_pair(0, (0,))
        copy_u(0, 0, False)
        quant_u(0, 0)
        for g in range(NPASS):
            if g + 1 < NPASS:
                tr_pair(0, (g + 1,))
                copy_u(0, g + 1, False)
            else:
                tr_pair(1, (0, 1))
            quant_pe(0, g)
            if g + 1 < NPASS:
                quant_u(0, g + 1)
            for t in range(4):
                s1_pass(0, 0, t, g)
        for t in range(4):
            s1_evac(0, 0, t, False)
        quant_pe(1, 0)
        quant_pe(1, 1)
        tr_pair(1, (2, 3))
        s1_copy(0, 0)
        quant_pe(1, 2)
        s1_quant(0, 0)
        quant_pe(1, 3)
        tr_pair(2, (0, 1))
        quant_pe(2, 0)
        quant_pe(2, 1)

        for n in range(1, NCHUNK):
            sorts(n + 2, (0, 1))
            s1_banks(0, n, (0, 1), False)
            if n + 1 < NCHUNK:
                tr_pair(n + 1, (2, 3))
                quant_pe(n + 1, 2)
                quant_pe(n + 1, 3)
            slot_copy(n)
            slot_load(n)
            sorts(n + 2, (2, 3))
            s1_banks(0, n, (2, 3), False)
            slot_copy_ahead(n)
            s1_copy(0, n)
            slot_quant(n)
            s1_quant(0, n)
            if n + 2 < NCHUNK:
                tr_pair(n + 2, (0, 1))
                quant_pe(n + 2, 0)
                quant_pe(n + 2, 1)

        for x in range(NCHUNK, NGROUP * NCHUNK):
            c = x // NCHUNK
            n = x % NCHUNK
            s1_banks(c, n, (0, 1, 2, 3), False)
            slot_copy_ahead(x)
            slot_copy(x)
            slot_load(x)
            s1_copy(c, n)
            slot_quant(x)
            s1_quant(c, n)

        def q_unit(idx):
            n = idx // NGROUP
            c = idx % NGROUP
            s1_banks(NGROUP + c, n, (0, 1, 2, 3), True)
            s1_copy(NGROUP + c, n)
            s1_quant(NGROUP + c, n)

        lead = NGROUP + 1
        for idx in range(lead):
            q_unit(idx)
        for i in range(4 * NCHUNK):
            s2_tile(i)
            if i + lead < NGROUP * NCHUNK:
                q_unit(i + lead)
